import numpy as np
import ml_dtypes

BF16 = ml_dtypes.bfloat16


def bf(x):
    return np.asarray(x, np.float32).astype(BF16)


def f32(x):
    return np.asarray(x, np.float32)


def f64(x):
    return np.asarray(x).astype(np.float64)


def striped(idx):
    return np.tile(idx.reshape(-1, 16).T, (8, 1))


V, E, D, DD, HID, RUN, K, N = 1024, 128, 128, 256, 512, 512, 12, 6144
LOG_DAMPING = -1.0
DT = 1.0
BIAS = 0.3


def sigmoid(v):
    return 1.0 / (1.0 + np.exp(-v))


def mlp_grad(x, w1, b1, w2):
    return w1 @ (sigmoid(w1.T @ x + b1) * w2)


def setup_inputs():
    context = bf(np.random.standard_normal((DD, N)))
    table = bf(np.random.standard_normal((V, E)))
    fw = bf(np.random.standard_normal((E, D)) / np.sqrt(E))
    fb = f32(BIAS * np.random.standard_normal((D, 1)))
    tw1 = bf(np.random.standard_normal((D, HID)) / np.sqrt(D))
    tb1 = f32(BIAS * np.random.standard_normal((HID, 1)))
    tw2 = f32(np.random.standard_normal((HID, 1)))
    vw1 = bf(np.random.standard_normal((D, HID)) / np.sqrt(D))
    vb1 = f32(BIAS * np.random.standard_normal((HID, 1)))
    vw2 = f32(np.random.standard_normal((HID, 1)))
    idx = np.concatenate([np.random.permutation(V)[:RUN] for _ in range(K)])
    return {"context": context, "table": table, "fw": fw, "fb": fb, "tw1": tw1, "tb1": tb1, "tw2": tw2, "vw1": vw1, "vb1": vb1, "vw2": vw2, "offs": striped(idx)}


def reference(context, table, fw, fb, tw1, tb1, tw2, vw1, vb1, vw2, offs):
    idx = offs[:16].T.reshape(-1)
    q, p = f64(context)[:D], f64(context)[D:]
    force = f64(fw).T @ f64(table)[idx].T + f64(fb)
    lam = np.exp(LOG_DAMPING)
    tw1, tb1, tw2 = f64(tw1), f64(tb1), f64(tw2)
    vw1, vb1, vw2 = f64(vw1), f64(vb1), f64(vw2)
    ph = p + DT / 2 * (-mlp_grad(q, vw1, vb1, vw2) - lam * mlp_grad(p, tw1, tb1, tw2) + force)
    dt_half = mlp_grad(ph, tw1, tb1, tw2)
    qn = q + DT * dt_half
    pn = ph + DT / 2 * (-mlp_grad(qn, vw1, vb1, vw2) - lam * dt_half + force)
    return np.concatenate([qn, pn], axis=0)

@@ -1,0 +1,171 @@
+import math
+from contextlib import ExitStack
+
+import concourse.mybir as mybir
+from concourse.masks import make_identity
+
+BF16, F32, U16 = mybir.dt.bfloat16, mybir.dt.float32, mybir.dt.uint16
+ADD, MULT = mybir.AluOpType.add, mybir.AluOpType.mult
+SIGMOID = mybir.ActivationFunctionType.Sigmoid
+IDENTITY = mybir.ActivationFunctionType.Identity
+
+P = 128
+ACTIONS = 1024
+HIDDEN = 512
+BLOCKS = HIDDEN // P
+TOKENS = 6144
+PIECE = 512
+PIECES = TOKENS // PIECE
+LAM = math.exp(-1.0)
+
+FLOPS = 2 * TOKENS * (P * P + 4 * 2 * P * HIDDEN)
+
+
+def tile_latenthamiltonianpredictor_b_kernel(
+    tc, context, table, fw, fb, tw1, tb1, tw2, vw1, vb1, vw2, offs, out
+):
+    nc = tc.nc
+    with ExitStack() as stack:
+        held = stack.enter_context(tc.tile_pool(name="held", bufs=1))
+
+        table_rows = held.tile([P, ACTIONS // P, P], BF16, name="table_rows")
+        nc.sync.dma_start(table_rows[:], table.rearrange("(a p) e -> p a e", p=P))
+        offsets = held.tile([P, TOKENS // 16], U16, name="offsets")
+        nc.sync.dma_start(offsets[:], offs)
+        q16 = [held.tile([P, PIECE], BF16, name=f"q16_{k}") for k in range(PIECES)]
+        p16 = [held.tile([P, PIECE], BF16, name=f"p16_{k}") for k in range(PIECES)]
+        for k in range(PIECES):
+            cols = slice(k * PIECE, (k + 1) * PIECE)
+            nc.sync.dma_start(p16[k][:], context[P : 2 * P, cols])
+            nc.sync.dma_start(q16[k][:], context[0:P, cols])
+
+        fw_in = held.tile([P, P], BF16, name="fw_in")
+        nc.scalar.dma_start(fw_in[:], fw)
+        fb_in = held.tile([P, 1], F32, name="fb_in")
+        nc.scalar.dma_start(fb_in[:], fb)
+        vw1_in = held.tile([P, HIDDEN], BF16, name="vw1_in")
+        nc.scalar.dma_start(vw1_in[:], vw1)
+        tw1_in = held.tile([P, HIDDEN], BF16, name="tw1_in")
+        nc.scalar.dma_start(tw1_in[:], tw1)
+        vb1_in = held.tile([P, BLOCKS], F32, name="vb1_in")
+        tb1_in = held.tile([P, BLOCKS], F32, name="tb1_in")
+        vw2_in = held.tile([P, BLOCKS], F32, name="vw2_in")
+        tw2_in = held.tile([P, BLOCKS], F32, name="tw2_in")
+        with nc.allow_non_contiguous_dma(reason="one float32 to a partition and block"):
+            for tile_in, vector in ((vb1_in, vb1), (tb1_in, tb1), (vw2_in, vw2), (tw2_in, tw2)):
+                nc.gpsimd.dma_start(tile_in[:], vector.rearrange("(a p) o -> p (a o)", p=P))
+
+        fw_half = held.tile([P, P], BF16, name="fw_half")
+        nc.vector.tensor_scalar(fw_half[:], fw_in[:], 0.5, None, op0=MULT)
+        fb_half = held.tile([P, 1], F32, name="fb_half")
+        nc.vector.tensor_scalar(fb_half[:], fb_in[:], 0.5, None, op0=MULT)
+        gate_kick_v = held.tile([P, BLOCKS], F32, name="gate_kick_v")
+        nc.vector.tensor_scalar(gate_kick_v[:], vw2_in[:], -0.5, None, op0=MULT)
+        gate_kick_t = held.tile([P, BLOCKS], F32, name="gate_kick_t")
+        nc.vector.tensor_scalar(gate_kick_t[:], tw2_in[:], -0.5 * LAM, None, op0=MULT)
+
+        identity = held.tile([P, P], BF16, name="identity")
+        make_identity(nc, identity[:])
+
+        table_cols = held.tile([P, ACTIONS], BF16, name="table_cols")
+        vw1_flipped = held.tile([P, HIDDEN], BF16, name="vw1_flipped")
+        tw1_flipped = held.tile([P, HIDDEN], BF16, name="tw1_flipped")
+        push = [held.tile([P, PIECE], F32, name=f"push_{k}") for k in range(PIECES)]
+        p_push = [held.tile([P, PIECE], F32, name=f"p_push_{k}") for k in range(PIECES)]
+
+        with (
+            tc.psum_pool(name="flips", bufs=1) as flips,
+            tc.psum_pool(name="forces", bufs=6) as forces,
+        ):
+            table_flip = flips.tile([P, ACTIONS], BF16, name="table_flip")
+            for a in range(ACTIONS // P):
+                nc.tensor.transpose(table_flip[:, a * P : (a + 1) * P], table_rows[:, a, :], identity[:])
+            nc.vector.tensor_copy(table_cols[:], table_flip[:])
+            w1_flip = flips.tile([P, 2 * HIDDEN], BF16, name="w1_flip")
+            for a in range(BLOCKS):
+                block = slice(a * P, (a + 1) * P)
+                nc.tensor.transpose(w1_flip[:, block], vw1_in[:, block], identity[:])
+                nc.tensor.transpose(
+                    w1_flip[:, HIDDEN + a * P : HIDDEN + (a + 1) * P], tw1_in[:, block], identity[:]
+                )
+            nc.vector.tensor_copy(vw1_flipped[:], w1_flip[:, 0:HIDDEN])
+            nc.vector.tensor_copy(tw1_flipped[:], w1_flip[:, HIDDEN : 2 * HIDDEN])
+
+            for k in range(PIECES):
+                force = forces.tile([P, PIECE], F32, name="force")
+                piece_offsets = offsets[:, k * (PIECE // 16) : (k + 1) * (PIECE // 16)]
+                nc.tensor.matmul(
+                    force[:], fw_half[:], table_cols[:].indirect(piece_offsets), start=True, stop=True
+                )
+                nc.scalar.activation(push[k][:], force[:], IDENTITY, bias=fb_half[:, 0:1])
+                nc.vector.scalar_tensor_tensor(
+                    p_push[k][:], force[:], fb_half[:, 0:1], p16[k][:], op0=ADD, op1=ADD
+                )
+
+        hiddens = stack.enter_context(tc.psum_pool(name="hiddens", bufs=5))
+        sums = stack.enter_context(tc.psum_pool(name="sums", bufs=3))
+        work = stack.enter_context(tc.tile_pool(name="work", bufs=4))
+        gates = stack.enter_context(tc.tile_pool(name="gates", bufs=12))
+        state = stack.enter_context(tc.tile_pool(name="state", bufs=3))
+
+        def add_gradient(total, x16, w1_in, b1_in, gate, w1_flipped, first, last):
+            gated_blocks = []
+            for a in range(BLOCKS):
+                hidden = hiddens.tile([P, PIECE], F32, name="hidden")
+                nc.tensor.matmul(hidden[:], w1_in[:, a * P : (a + 1) * P], x16, start=True, stop=True)
+                sig = work.tile([P, PIECE], F32, name="sig")
+                nc.scalar.activation(sig[:], hidden[:], SIGMOID, bias=b1_in[:, a : a + 1])
+                gated = gates.tile([P, PIECE], BF16, name="gated")
+                nc.vector.tensor_scalar(gated[:], sig[:], gate[:, a : a + 1], None, op0=MULT)
+                gated_blocks.append(gated)
+            for a in range(BLOCKS):
+                nc.tensor.matmul(
+                    total[:],
+                    w1_flipped[:, a * P : (a + 1) * P],
+                    gated_blocks[a][:],
+                    start=first and a == 0,
+                    stop=last and a == BLOCKS - 1,
+                )
+
+        ph16, ph_push, qn16, rest = {}, {}, {}, {}
+
+        def first_kick(k):
+            kick = sums.tile([P, PIECE], F32, name="kick", tag="sum")
+            add_gradient(kick, q16[k][:], vw1_in, vb1_in, gate_kick_v, vw1_flipped, True, False)
+            add_gradient(kick, p16[k][:], tw1_in, tb1_in, gate_kick_t, tw1_flipped, False, True)
+            ph32 = state.tile([P, PIECE], F32, name="ph32")
+            nc.vector.tensor_tensor(ph32[:], kick[:], p_push[k][:], ADD)
+            ph16_k = state.tile([P, PIECE], BF16, name="ph16_k")
+            nc.vector.tensor_copy(ph16_k[:], ph32[:])
+            ph_push_k = state.tile([P, PIECE], F32, name="ph_push_k")
+            nc.gpsimd.tensor_tensor(ph_push_k[:], ph32[:], push[k][:], ADD)
+            ph16[k], ph_push[k] = ph16_k, ph_push_k
+
+        def drift(k):
+            speed = sums.tile([P, PIECE], F32, name="speed", tag="sum")
+            add_gradient(speed, ph16[k][:], tw1_in, tb1_in, tw2_in, tw1_flipped, True, True)
+            qn32 = state.tile([P, PIECE], F32, name="qn32")
+            nc.vector.tensor_tensor(qn32[:], speed[:], q16[k][:], ADD)
+            nc.sync.dma_start(out[0:P, k * PIECE : (k + 1) * PIECE], qn32[:])
+            qn16_k = state.tile([P, PIECE], BF16, name="qn16_k")
+            nc.vector.tensor_copy(qn16_k[:], qn32[:])
+            rest_k = state.tile([P, PIECE], F32, name="rest_k")
+            nc.vector.scalar_tensor_tensor(
+                rest_k[:], speed[:], -0.5 * LAM, ph_push[k][:], op0=MULT, op1=ADD
+            )
+            qn16[k], rest[k] = qn16_k, rest_k
+
+        def second_kick(k):
+            kick = sums.tile([P, PIECE], F32, name="kick", tag="sum")
+            add_gradient(kick, qn16[k][:], vw1_in, vb1_in, gate_kick_v, vw1_flipped, True, True)
+            pn32 = state.tile([P, PIECE], F32, name="pn32")
+            nc.vector.tensor_tensor(pn32[:], kick[:], rest[k][:], ADD)
+            nc.sync.dma_start(out[P : 2 * P, k * PIECE : (k + 1) * PIECE], pn32[:])
+
+        for step in range(PIECES + 2):
+            if step < PIECES:
+                first_kick(step)
+            if 1 <= step <= PIECES:
+                drift(step - 1)
+            if step >= 2:
+                second_kick(step - 2)

@@ -7,7 +7,6 @@ from concourse.masks import make_identity
 BF16, F32, U16 = mybir.dt.bfloat16, mybir.dt.float32, mybir.dt.uint16
 ADD, MULT = mybir.AluOpType.add, mybir.AluOpType.mult
 SIGMOID = mybir.ActivationFunctionType.Sigmoid
-IDENTITY = mybir.ActivationFunctionType.Identity
 
 P = 128
 ACTIONS = 1024
@@ -27,33 +26,44 @@ def tile_latenthamiltonianpredictor_b_kernel(
     nc = tc.nc
     with ExitStack() as stack:
         held = stack.enter_context(tc.tile_pool(name="held", bufs=1))
+        forces = stack.enter_context(tc.psum_pool(name="forces", bufs=1))
+        hiddens = stack.enter_context(tc.psum_pool(name="hiddens", bufs=4))
+        sums = stack.enter_context(tc.psum_pool(name="sums", bufs=2))
+        sigmoids = stack.enter_context(tc.tile_pool(name="sigmoids", bufs=12))
+        state = stack.enter_context(tc.tile_pool(name="state", bufs=3))
+
+        identity = held.tile([P, P], BF16, name="identity")
+        make_identity(nc, identity[:])
 
         table_rows = held.tile([P, ACTIONS // P, P], BF16, name="table_rows")
         nc.sync.dma_start(table_rows[:], table.rearrange("(a p) e -> p a e", p=P))
         offsets = held.tile([P, TOKENS // 16], U16, name="offsets")
         nc.sync.dma_start(offsets[:], offs)
-        q16 = [held.tile([P, PIECE], BF16, name=f"q16_{k}") for k in range(PIECES)]
-        p16 = [held.tile([P, PIECE], BF16, name=f"p16_{k}") for k in range(PIECES)]
-        for k in range(PIECES):
-            cols = slice(k * PIECE, (k + 1) * PIECE)
-            nc.sync.dma_start(p16[k][:], context[P : 2 * P, cols])
-            nc.sync.dma_start(q16[k][:], context[0:P, cols])
-
-        fw_in = held.tile([P, P], BF16, name="fw_in")
-        nc.scalar.dma_start(fw_in[:], fw)
-        fb_in = held.tile([P, 1], F32, name="fb_in")
-        nc.scalar.dma_start(fb_in[:], fb)
         vw1_in = held.tile([P, HIDDEN], BF16, name="vw1_in")
         nc.scalar.dma_start(vw1_in[:], vw1)
-        tw1_in = held.tile([P, HIDDEN], BF16, name="tw1_in")
-        nc.scalar.dma_start(tw1_in[:], tw1)
+        q16 = [held.tile([P, PIECE], BF16, name=f"q16_{k}") for k in range(PIECES)]
+        p16 = [held.tile([P, PIECE], BF16, name=f"p16_{k}") for k in range(PIECES)]
+        nc.scalar.dma_start(q16[0][:], context[0:P, 0:PIECE])
         vb1_in = held.tile([P, BLOCKS], F32, name="vb1_in")
         tb1_in = held.tile([P, BLOCKS], F32, name="tb1_in")
         vw2_in = held.tile([P, BLOCKS], F32, name="vw2_in")
         tw2_in = held.tile([P, BLOCKS], F32, name="tw2_in")
+        tw1_in = held.tile([P, HIDDEN], BF16, name="tw1_in")
+        fw_in = held.tile([P, P], BF16, name="fw_in")
+        fb_in = held.tile([P, 1], F32, name="fb_in")
         with nc.allow_non_contiguous_dma(reason="one float32 to a partition and block"):
-            for tile_in, vector in ((vb1_in, vb1), (tb1_in, tb1), (vw2_in, vw2), (tw2_in, tw2)):
-                nc.gpsimd.dma_start(tile_in[:], vector.rearrange("(a p) o -> p (a o)", p=P))
+            nc.scalar.dma_start(vb1_in[:], vb1.rearrange("(a p) o -> p (a o)", p=P))
+            nc.scalar.dma_start(vw2_in[:], vw2.rearrange("(a p) o -> p (a o)", p=P))
+            nc.scalar.dma_start(tw1_in[:], tw1)
+            nc.scalar.dma_start(tb1_in[:], tb1.rearrange("(a p) o -> p (a o)", p=P))
+            nc.scalar.dma_start(tw2_in[:], tw2.rearrange("(a p) o -> p (a o)", p=P))
+        nc.sync.dma_start(fw_in[:], fw)
+        nc.sync.dma_start(fb_in[:], fb)
+        for k in range(PIECES):
+            cols = slice(k * PIECE, (k + 1) * PIECE)
+            nc.sync.dma_start(p16[k][:], context[P : 2 * P, cols])
+            if k > 0:
+                nc.sync.dma_start(q16[k][:], context[0:P, cols])
 
         fw_half = held.tile([P, P], BF16, name="fw_half")
         nc.vector.tensor_scalar(fw_half[:], fw_in[:], 0.5, None, op0=MULT)
@@ -64,107 +74,95 @@ def tile_latenthamiltonianpredictor_b_kernel(
         gate_kick_t = held.tile([P, BLOCKS], F32, name="gate_kick_t")
         nc.vector.tensor_scalar(gate_kick_t[:], tw2_in[:], -0.5 * LAM, None, op0=MULT)
 
-        identity = held.tile([P, P], BF16, name="identity")
-        make_identity(nc, identity[:])
-
         table_cols = held.tile([P, ACTIONS], BF16, name="table_cols")
-        vw1_flipped = held.tile([P, HIDDEN], BF16, name="vw1_flipped")
-        tw1_flipped = held.tile([P, HIDDEN], BF16, name="tw1_flipped")
-        push = [held.tile([P, PIECE], F32, name=f"push_{k}") for k in range(PIECES)]
-        p_push = [held.tile([P, PIECE], F32, name=f"p_push_{k}") for k in range(PIECES)]
+        table_flip = sums.tile([P, ACTIONS], BF16, name="table_flip", tag="sum")
+        for a in range(ACTIONS // P):
+            nc.tensor.transpose(table_flip[:, a * P : (a + 1) * P], table_rows[:, a, :], identity[:])
+        nc.vector.tensor_copy(table_cols[:], table_flip[:])
 
-        with (
-            tc.psum_pool(name="flips", bufs=1) as flips,
-            tc.psum_pool(name="forces", bufs=6) as forces,
-        ):
-            table_flip = flips.tile([P, ACTIONS], BF16, name="table_flip")
-            for a in range(ACTIONS // P):
-                nc.tensor.transpose(table_flip[:, a * P : (a + 1) * P], table_rows[:, a, :], identity[:])
-            nc.vector.tensor_copy(table_cols[:], table_flip[:])
-            w1_flip = flips.tile([P, 2 * HIDDEN], BF16, name="w1_flip")
-            for a in range(BLOCKS):
-                block = slice(a * P, (a + 1) * P)
-                nc.tensor.transpose(w1_flip[:, block], vw1_in[:, block], identity[:])
-                nc.tensor.transpose(
-                    w1_flip[:, HIDDEN + a * P : HIDDEN + (a + 1) * P], tw1_in[:, block], identity[:]
-                )
-            nc.vector.tensor_copy(vw1_flipped[:], w1_flip[:, 0:HIDDEN])
-            nc.vector.tensor_copy(tw1_flipped[:], w1_flip[:, HIDDEN : 2 * HIDDEN])
+        w1_flip = sums.tile([P, 2 * HIDDEN], BF16, name="w1_flip", tag="sum")
+        kick_v_out = held.tile([P, HIDDEN], BF16, name="kick_v_out")
+        kick_t_out = held.tile([P, HIDDEN], BF16, name="kick_t_out")
+        drift_t_out = held.tile([P, HIDDEN], BF16, name="drift_t_out")
+        for a in range(BLOCKS):
+            block = slice(a * P, (a + 1) * P)
+            nc.tensor.transpose(w1_flip[:, block], vw1_in[:, block], identity[:])
+            nc.vector.tensor_scalar(kick_v_out[:, block], w1_flip[:, block], gate_kick_v[:, a : a + 1], None, op0=MULT)
+        for a in range(BLOCKS):
+            block = slice(a * P, (a + 1) * P)
+            t_block = slice(HIDDEN + a * P, HIDDEN + (a + 1) * P)
+            nc.tensor.transpose(w1_flip[:, t_block], tw1_in[:, block], identity[:])
+            nc.vector.tensor_scalar(kick_t_out[:, block], w1_flip[:, t_block], gate_kick_t[:, a : a + 1], None, op0=MULT)
+            nc.vector.tensor_scalar(drift_t_out[:, block], w1_flip[:, t_block], tw2_in[:, a : a + 1], None, op0=MULT)
 
-            for k in range(PIECES):
-                force = forces.tile([P, PIECE], F32, name="force")
-                piece_offsets = offsets[:, k * (PIECE // 16) : (k + 1) * (PIECE // 16)]
-                nc.tensor.matmul(
-                    force[:], fw_half[:], table_cols[:].indirect(piece_offsets), start=True, stop=True
-                )
-                nc.scalar.activation(push[k][:], force[:], IDENTITY, bias=fb_half[:, 0:1])
-                nc.vector.scalar_tensor_tensor(
-                    p_push[k][:], force[:], fb_half[:, 0:1], p16[k][:], op0=ADD, op1=ADD
-                )
-
-        hiddens = stack.enter_context(tc.psum_pool(name="hiddens", bufs=5))
-        sums = stack.enter_context(tc.psum_pool(name="sums", bufs=3))
-        work = stack.enter_context(tc.tile_pool(name="work", bufs=4))
-        gates = stack.enter_context(tc.tile_pool(name="gates", bufs=12))
-        state = stack.enter_context(tc.tile_pool(name="state", bufs=3))
-
-        def add_gradient(total, x16, w1_in, b1_in, gate, w1_flipped, first, last):
-            gated_blocks = []
+        def add_gradient(total, x16, w1_in, b1_in, w_out, first, last):
+            sig_blocks = []
             for a in range(BLOCKS):
                 hidden = hiddens.tile([P, PIECE], F32, name="hidden")
                 nc.tensor.matmul(hidden[:], w1_in[:, a * P : (a + 1) * P], x16, start=True, stop=True)
-                sig = work.tile([P, PIECE], F32, name="sig")
+                sig = sigmoids.tile([P, PIECE], BF16, name="sig")
                 nc.scalar.activation(sig[:], hidden[:], SIGMOID, bias=b1_in[:, a : a + 1])
-                gated = gates.tile([P, PIECE], BF16, name="gated")
-                nc.vector.tensor_scalar(gated[:], sig[:], gate[:, a : a + 1], None, op0=MULT)
-                gated_blocks.append(gated)
+                sig_blocks.append(sig)
             for a in range(BLOCKS):
                 nc.tensor.matmul(
                     total[:],
-                    w1_flipped[:, a * P : (a + 1) * P],
-                    gated_blocks[a][:],
+                    w_out[:, a * P : (a + 1) * P],
+                    sig_blocks[a][:],
                     start=first and a == 0,
                     stop=last and a == BLOCKS - 1,
                 )
 
-        ph16, ph_push, qn16, rest = {}, {}, {}, {}
+        half_force, ph16, ph_push, qn16, rest = {}, {}, {}, {}, {}
+
+        def look_up(pair):
+            force = forces.tile([P, 2, PIECE], F32, name="force")
+            for i in range(2):
+                k = 2 * pair + i
+                piece_offsets = offsets[:, k * (PIECE // 16) : (k + 1) * (PIECE // 16)]
+                nc.tensor.matmul(
+                    force[:, i, :], fw_half[:], table_cols[:].indirect(piece_offsets), start=True, stop=True
+                )
+                half_force[k] = force[:, i, :]
 
         def first_kick(k):
             kick = sums.tile([P, PIECE], F32, name="kick", tag="sum")
-            add_gradient(kick, q16[k][:], vw1_in, vb1_in, gate_kick_v, vw1_flipped, True, False)
-            add_gradient(kick, p16[k][:], tw1_in, tb1_in, gate_kick_t, tw1_flipped, False, True)
+            add_gradient(kick, q16[k][:], vw1_in, vb1_in, kick_v_out, True, False)
+            add_gradient(kick, p16[k][:], tw1_in, tb1_in, kick_t_out, False, True)
+            unforced = state.tile([P, PIECE], F32, name="unforced")
+            nc.vector.tensor_tensor(unforced[:], kick[:], p16[k][:], ADD)
             ph32 = state.tile([P, PIECE], F32, name="ph32")
-            nc.vector.tensor_tensor(ph32[:], kick[:], p_push[k][:], ADD)
+            nc.vector.scalar_tensor_tensor(ph32[:], half_force[k], fb_half[:, 0:1], unforced[:], op0=ADD, op1=ADD)
             ph16_k = state.tile([P, PIECE], BF16, name="ph16_k")
             nc.vector.tensor_copy(ph16_k[:], ph32[:])
             ph_push_k = state.tile([P, PIECE], F32, name="ph_push_k")
-            nc.gpsimd.tensor_tensor(ph_push_k[:], ph32[:], push[k][:], ADD)
+            nc.vector.scalar_tensor_tensor(ph_push_k[:], half_force[k], fb_half[:, 0:1], ph32[:], op0=ADD, op1=ADD)
             ph16[k], ph_push[k] = ph16_k, ph_push_k
 
         def drift(k):
             speed = sums.tile([P, PIECE], F32, name="speed", tag="sum")
-            add_gradient(speed, ph16[k][:], tw1_in, tb1_in, tw2_in, tw1_flipped, True, True)
+            add_gradient(speed, ph16[k][:], tw1_in, tb1_in, drift_t_out, True, True)
             qn32 = state.tile([P, PIECE], F32, name="qn32")
             nc.vector.tensor_tensor(qn32[:], speed[:], q16[k][:], ADD)
             nc.sync.dma_start(out[0:P, k * PIECE : (k + 1) * PIECE], qn32[:])
             qn16_k = state.tile([P, PIECE], BF16, name="qn16_k")
             nc.vector.tensor_copy(qn16_k[:], qn32[:])
             rest_k = state.tile([P, PIECE], F32, name="rest_k")
-            nc.vector.scalar_tensor_tensor(
-                rest_k[:], speed[:], -0.5 * LAM, ph_push[k][:], op0=MULT, op1=ADD
-            )
+            nc.vector.scalar_tensor_tensor(rest_k[:], speed[:], -0.5 * LAM, ph_push[k][:], op0=MULT, op1=ADD)
             qn16[k], rest[k] = qn16_k, rest_k
 
         def second_kick(k):
             kick = sums.tile([P, PIECE], F32, name="kick", tag="sum")
-            add_gradient(kick, qn16[k][:], vw1_in, vb1_in, gate_kick_v, vw1_flipped, True, True)
+            add_gradient(kick, qn16[k][:], vw1_in, vb1_in, kick_v_out, True, True)
             pn32 = state.tile([P, PIECE], F32, name="pn32")
             nc.vector.tensor_tensor(pn32[:], kick[:], rest[k][:], ADD)
             nc.sync.dma_start(out[P : 2 * P, k * PIECE : (k + 1) * PIECE], pn32[:])
 
+        look_up(0)
         for step in range(PIECES + 2):
             if step < PIECES:
                 first_kick(step)
+            if step % 2 == 1 and step + 1 < PIECES:
+                look_up((step + 1) // 2)
             if 1 <= step <= PIECES:
                 drift(step - 1)
             if step >= 2:

@@ -29,41 +29,43 @@ def tile_latenthamiltonianpredictor_b_kernel(
         forces = stack.enter_context(tc.psum_pool(name="forces", bufs=1))
         hiddens = stack.enter_context(tc.psum_pool(name="hiddens", bufs=4))
         sums = stack.enter_context(tc.psum_pool(name="sums", bufs=2))
-        sigmoids = stack.enter_context(tc.tile_pool(name="sigmoids", bufs=12))
+        sigmoids = stack.enter_context(tc.tile_pool(name="sigmoids", bufs=20))
         state = stack.enter_context(tc.tile_pool(name="state", bufs=3))
 
         identity = held.tile([P, P], BF16, name="identity")
         make_identity(nc, identity[:])
 
-        table_rows = held.tile([P, ACTIONS // P, P], BF16, name="table_rows")
-        nc.sync.dma_start(table_rows[:], table.rearrange("(a p) e -> p a e", p=P))
-        offsets = held.tile([P, TOKENS // 16], U16, name="offsets")
-        nc.sync.dma_start(offsets[:], offs)
-        vw1_in = held.tile([P, HIDDEN], BF16, name="vw1_in")
-        nc.scalar.dma_start(vw1_in[:], vw1)
         q16 = [held.tile([P, PIECE], BF16, name=f"q16_{k}") for k in range(PIECES)]
         p16 = [held.tile([P, PIECE], BF16, name=f"p16_{k}") for k in range(PIECES)]
-        nc.scalar.dma_start(q16[0][:], context[0:P, 0:PIECE])
+        table_rows = held.tile([P, ACTIONS // P, P], BF16, name="table_rows")
+        offsets = held.tile([P, TOKENS // 16], U16, name="offsets")
+        fw_in = held.tile([P, P], BF16, name="fw_in")
+        fb_in = held.tile([P, 1], F32, name="fb_in")
+        nc.sync.dma_start(q16[0][:], context[0:P, 0:PIECE])
+        nc.sync.dma_start(p16[0][:], context[P : 2 * P, 0:PIECE])
+        nc.sync.dma_start(table_rows[:], table.rearrange("(a p) e -> p a e", p=P))
+        nc.sync.dma_start(offsets[:], offs)
+        nc.sync.dma_start(fw_in[:], fw)
+        nc.sync.dma_start(fb_in[:], fb)
+        for k in range(1, PIECES):
+            cols = slice(k * PIECE, (k + 1) * PIECE)
+            nc.sync.dma_start(q16[k][:], context[0:P, cols])
+            nc.sync.dma_start(p16[k][:], context[P : 2 * P, cols])
+
+        vw1_in = held.tile([P, HIDDEN], BF16, name="vw1_in")
+        tw1_in = held.tile([P, HIDDEN], BF16, name="tw1_in")
         vb1_in = held.tile([P, BLOCKS], F32, name="vb1_in")
         tb1_in = held.tile([P, BLOCKS], F32, name="tb1_in")
         vw2_in = held.tile([P, BLOCKS], F32, name="vw2_in")
         tw2_in = held.tile([P, BLOCKS], F32, name="tw2_in")
-        tw1_in = held.tile([P, HIDDEN], BF16, name="tw1_in")
-        fw_in = held.tile([P, P], BF16, name="fw_in")
-        fb_in = held.tile([P, 1], F32, name="fb_in")
-        with nc.allow_non_contiguous_dma(reason="one float32 to a partition and block"):
-            nc.scalar.dma_start(vb1_in[:], vb1.rearrange("(a p) o -> p (a o)", p=P))
-            nc.scalar.dma_start(vw2_in[:], vw2.rearrange("(a p) o -> p (a o)", p=P))
-            nc.scalar.dma_start(tw1_in[:], tw1)
-            nc.scalar.dma_start(tb1_in[:], tb1.rearrange("(a p) o -> p (a o)", p=P))
-            nc.scalar.dma_start(tw2_in[:], tw2.rearrange("(a p) o -> p (a o)", p=P))
-        nc.sync.dma_start(fw_in[:], fw)
-        nc.sync.dma_start(fb_in[:], fb)
-        for k in range(PIECES):
-            cols = slice(k * PIECE, (k + 1) * PIECE)
-            nc.sync.dma_start(p16[k][:], context[P : 2 * P, cols])
-            if k > 0:
-                nc.sync.dma_start(q16[k][:], context[0:P, cols])
+        nc.scalar.dma_start(vw1_in[:], vw1)
+        nc.scalar.dma_start(vb1_in[:], vb1.rearrange("(p a) o -> p (a o)", a=BLOCKS))
+        nc.scalar.dma_start(tw1_in[:], tw1)
+        nc.scalar.dma_start(tb1_in[:], tb1.rearrange("(p a) o -> p (a o)", a=BLOCKS))
+        nc.scalar.dma_start(vw2_in[:], vw2.rearrange("(p a) o -> p (a o)", a=BLOCKS))
+        nc.scalar.dma_start(tw2_in[:], tw2.rearrange("(p a) o -> p (a o)", a=BLOCKS))
+        vw1_blocks = vw1_in[:].rearrange("d (p a) -> d a p", a=BLOCKS)
+        tw1_blocks = tw1_in[:].rearrange("d (p a) -> d a p", a=BLOCKS)
 
         fw_half = held.tile([P, P], BF16, name="fw_half")
         nc.vector.tensor_scalar(fw_half[:], fw_in[:], 0.5, None, op0=MULT)
@@ -74,35 +76,38 @@ def tile_latenthamiltonianpredictor_b_kernel(
         gate_kick_t = held.tile([P, BLOCKS], F32, name="gate_kick_t")
         nc.vector.tensor_scalar(gate_kick_t[:], tw2_in[:], -0.5 * LAM, None, op0=MULT)
 
-        table_cols = held.tile([P, ACTIONS], BF16, name="table_cols")
-        table_flip = sums.tile([P, ACTIONS], BF16, name="table_flip", tag="sum")
-        for a in range(ACTIONS // P):
-            nc.tensor.transpose(table_flip[:, a * P : (a + 1) * P], table_rows[:, a, :], identity[:])
-        nc.vector.tensor_copy(table_cols[:], table_flip[:])
-
         w1_flip = sums.tile([P, 2 * HIDDEN], BF16, name="w1_flip", tag="sum")
         kick_v_out = held.tile([P, HIDDEN], BF16, name="kick_v_out")
         kick_t_out = held.tile([P, HIDDEN], BF16, name="kick_t_out")
         drift_t_out = held.tile([P, HIDDEN], BF16, name="drift_t_out")
         for a in range(BLOCKS):
             block = slice(a * P, (a + 1) * P)
-            nc.tensor.transpose(w1_flip[:, block], vw1_in[:, block], identity[:])
+            nc.tensor.transpose(w1_flip[:, block], vw1_blocks[:, a, :], identity[:])
             nc.vector.tensor_scalar(kick_v_out[:, block], w1_flip[:, block], gate_kick_v[:, a : a + 1], None, op0=MULT)
         for a in range(BLOCKS):
             block = slice(a * P, (a + 1) * P)
             t_block = slice(HIDDEN + a * P, HIDDEN + (a + 1) * P)
-            nc.tensor.transpose(w1_flip[:, t_block], tw1_in[:, block], identity[:])
+            nc.tensor.transpose(w1_flip[:, t_block], tw1_blocks[:, a, :], identity[:])
             nc.vector.tensor_scalar(kick_t_out[:, block], w1_flip[:, t_block], gate_kick_t[:, a : a + 1], None, op0=MULT)
             nc.vector.tensor_scalar(drift_t_out[:, block], w1_flip[:, t_block], tw2_in[:, a : a + 1], None, op0=MULT)
 
-        def add_gradient(total, x16, w1_in, b1_in, w_out, first, last):
+        table_flip = forces.tile([P, ACTIONS], BF16, name="table_flip", tag="force")
+        table_cols = held.tile([P, ACTIONS], BF16, name="table_cols")
+        for a in range(ACTIONS // P):
+            nc.tensor.transpose(table_flip[:, a * P : (a + 1) * P], table_rows[:, a, :], identity[:])
+        nc.vector.tensor_copy(table_cols[:], table_flip[:])
+
+        def hidden_layer(x16, w1_blocks, b1_in):
             sig_blocks = []
             for a in range(BLOCKS):
                 hidden = hiddens.tile([P, PIECE], F32, name="hidden")
-                nc.tensor.matmul(hidden[:], w1_in[:, a * P : (a + 1) * P], x16, start=True, stop=True)
+                nc.tensor.matmul(hidden[:], w1_blocks[:, a, :], x16, start=True, stop=True)
                 sig = sigmoids.tile([P, PIECE], BF16, name="sig")
                 nc.scalar.activation(sig[:], hidden[:], SIGMOID, bias=b1_in[:, a : a + 1])
                 sig_blocks.append(sig)
+            return sig_blocks
+
+        def add_output(total, w_out, sig_blocks, first, last):
             for a in range(BLOCKS):
                 nc.tensor.matmul(
                     total[:],
@@ -124,10 +129,13 @@ def tile_latenthamiltonianpredictor_b_kernel(
                 )
                 half_force[k] = force[:, i, :]
 
-        def first_kick(k):
+        def start_first_kick(k):
+            return hidden_layer(q16[k][:], vw1_blocks, vb1_in) + hidden_layer(p16[k][:], tw1_blocks, tb1_in)
+
+        def finish_first_kick(k, sig_blocks):
             kick = sums.tile([P, PIECE], F32, name="kick", tag="sum")
-            add_gradient(kick, q16[k][:], vw1_in, vb1_in, kick_v_out, True, False)
-            add_gradient(kick, p16[k][:], tw1_in, tb1_in, kick_t_out, False, True)
+            add_output(kick, kick_v_out, sig_blocks[:BLOCKS], True, False)
+            add_output(kick, kick_t_out, sig_blocks[BLOCKS:], False, True)
             unforced = state.tile([P, PIECE], F32, name="unforced")
             nc.vector.tensor_tensor(unforced[:], kick[:], p16[k][:], ADD)
             ph32 = state.tile([P, PIECE], F32, name="ph32")
@@ -137,10 +145,15 @@ def tile_latenthamiltonianpredictor_b_kernel(
             ph_push_k = state.tile([P, PIECE], F32, name="ph_push_k")
             nc.vector.scalar_tensor_tensor(ph_push_k[:], half_force[k], fb_half[:, 0:1], ph32[:], op0=ADD, op1=ADD)
             ph16[k], ph_push[k] = ph16_k, ph_push_k
+            if k % 2 == 1 and k + 1 < PIECES:
+                look_up((k + 1) // 2)
 
-        def drift(k):
+        def start_drift(k):
+            return hidden_layer(ph16[k][:], tw1_blocks, tb1_in)
+
+        def finish_drift(k, sig_blocks):
             speed = sums.tile([P, PIECE], F32, name="speed", tag="sum")
-            add_gradient(speed, ph16[k][:], tw1_in, tb1_in, drift_t_out, True, True)
+            add_output(speed, drift_t_out, sig_blocks, True, True)
             qn32 = state.tile([P, PIECE], F32, name="qn32")
             nc.vector.tensor_tensor(qn32[:], speed[:], q16[k][:], ADD)
             nc.sync.dma_start(out[0:P, k * PIECE : (k + 1) * PIECE], qn32[:])
@@ -150,20 +163,31 @@ def tile_latenthamiltonianpredictor_b_kernel(
             nc.vector.scalar_tensor_tensor(rest_k[:], speed[:], -0.5 * LAM, ph_push[k][:], op0=MULT, op1=ADD)
             qn16[k], rest[k] = qn16_k, rest_k
 
-        def second_kick(k):
+        def start_second_kick(k):
+            return hidden_layer(qn16[k][:], vw1_blocks, vb1_in)
+
+        def finish_second_kick(k, sig_blocks):
             kick = sums.tile([P, PIECE], F32, name="kick", tag="sum")
-            add_gradient(kick, qn16[k][:], vw1_in, vb1_in, kick_v_out, True, True)
+            add_output(kick, kick_v_out, sig_blocks, True, True)
             pn32 = state.tile([P, PIECE], F32, name="pn32")
             nc.vector.tensor_tensor(pn32[:], kick[:], rest[k][:], ADD)
             nc.sync.dma_start(out[P : 2 * P, k * PIECE : (k + 1) * PIECE], pn32[:])
 
+        unfinished = []
+
+        def run_stage(start, finish, k):
+            sig_blocks = start(k)
+            for finish_last, k_last, sig_blocks_last in unfinished:
+                finish_last(k_last, sig_blocks_last)
+            unfinished.clear()
+            unfinished.append((finish, k, sig_blocks))
+
         look_up(0)
         for step in range(PIECES + 2):
             if step < PIECES:
-                first_kick(step)
-            if step % 2 == 1 and step + 1 < PIECES:
-                look_up((step + 1) // 2)
+                run_stage(start_first_kick, finish_first_kick, step)
             if 1 <= step <= PIECES:
-                drift(step - 1)
+                run_stage(start_drift, finish_drift, step - 1)
             if step >= 2:
-                second_kick(step - 2)
+                run_stage(start_second_kick, finish_second_kick, step - 2)
+        finish_second_kick(PIECES - 1, unfinished[0][2])

@@ -97,18 +97,10 @@ def tile_latenthamiltonianpredictor_b_kernel(
             nc.tensor.transpose(table_flip[:, a * P : (a + 1) * P], table_rows[:, a, :], identity[:])
         nc.vector.tensor_copy(table_cols[:], table_flip[:])
 
-        def hidden_layer(x16, w1_blocks, b1_in):
-            sig_blocks = []
-            for a in range(BLOCKS):
-                hidden = hiddens.tile([P, PIECE], F32, name="hidden")
-                nc.tensor.matmul(hidden[:], w1_blocks[:, a, :], x16, start=True, stop=True)
-                sig = sigmoids.tile([P, PIECE], BF16, name="sig")
-                nc.scalar.activation(sig[:], hidden[:], SIGMOID, bias=b1_in[:, a : a + 1])
-                sig_blocks.append(sig)
-            return sig_blocks
+        waiting = []
 
-        def add_output(total, w_out, sig_blocks, first, last):
-            for a in range(BLOCKS):
+        def output_block(a):
+            for sig_blocks, total, w_out, first, last, after in waiting:
                 nc.tensor.matmul(
                     total[:],
                     w_out[:, a * P : (a + 1) * P],
@@ -116,6 +108,26 @@ def tile_latenthamiltonianpredictor_b_kernel(
                     start=first and a == 0,
                     stop=last and a == BLOCKS - 1,
                 )
+
+        def close_unit():
+            for sig_blocks, total, w_out, first, last, after in waiting:
+                after()
+            waiting.clear()
+
+        def add_gradient(total, x16, w1_blocks, b1_in, w_out, first, last, after):
+            sig_blocks = []
+            for a in range(BLOCKS):
+                hidden = hiddens.tile([P, PIECE], F32, name="hidden")
+                nc.tensor.matmul(hidden[:], w1_blocks[:, a, :], x16, start=True, stop=True)
+                sig = sigmoids.tile([P, PIECE], BF16, name="sig")
+                nc.scalar.activation(sig[:], hidden[:], SIGMOID, bias=b1_in[:, a : a + 1])
+                sig_blocks.append(sig)
+                output_block(a)
+            close_unit()
+            waiting.append((sig_blocks, total, w_out, first, last, after))
+
+        def nothing():
+            return None
 
         half_force, ph16, ph_push, qn16, rest = {}, {}, {}, {}, {}
 
@@ -129,65 +141,58 @@ def tile_latenthamiltonianpredictor_b_kernel(
                 )
                 half_force[k] = force[:, i, :]
 
-        def start_first_kick(k):
-            return hidden_layer(q16[k][:], vw1_blocks, vb1_in) + hidden_layer(p16[k][:], tw1_blocks, tb1_in)
-
-        def finish_first_kick(k, sig_blocks):
+        def first_kick(k):
             kick = sums.tile([P, PIECE], F32, name="kick", tag="sum")
-            add_output(kick, kick_v_out, sig_blocks[:BLOCKS], True, False)
-            add_output(kick, kick_t_out, sig_blocks[BLOCKS:], False, True)
-            unforced = state.tile([P, PIECE], F32, name="unforced")
-            nc.vector.tensor_tensor(unforced[:], kick[:], p16[k][:], ADD)
-            ph32 = state.tile([P, PIECE], F32, name="ph32")
-            nc.vector.scalar_tensor_tensor(ph32[:], half_force[k], fb_half[:, 0:1], unforced[:], op0=ADD, op1=ADD)
-            ph16_k = state.tile([P, PIECE], BF16, name="ph16_k")
-            nc.vector.tensor_copy(ph16_k[:], ph32[:])
-            ph_push_k = state.tile([P, PIECE], F32, name="ph_push_k")
-            nc.vector.scalar_tensor_tensor(ph_push_k[:], half_force[k], fb_half[:, 0:1], ph32[:], op0=ADD, op1=ADD)
-            ph16[k], ph_push[k] = ph16_k, ph_push_k
-            if k % 2 == 1 and k + 1 < PIECES:
-                look_up((k + 1) // 2)
 
-        def start_drift(k):
-            return hidden_layer(ph16[k][:], tw1_blocks, tb1_in)
+            def finish():
+                unforced = state.tile([P, PIECE], F32, name="unforced")
+                nc.vector.tensor_tensor(unforced[:], kick[:], p16[k][:], ADD)
+                ph32 = state.tile([P, PIECE], F32, name="ph32")
+                nc.vector.scalar_tensor_tensor(ph32[:], half_force[k], fb_half[:, 0:1], unforced[:], op0=ADD, op1=ADD)
+                ph16_k = state.tile([P, PIECE], BF16, name="ph16_k")
+                nc.vector.tensor_copy(ph16_k[:], ph32[:])
+                ph_push_k = state.tile([P, PIECE], F32, name="ph_push_k")
+                nc.vector.scalar_tensor_tensor(ph_push_k[:], half_force[k], fb_half[:, 0:1], ph32[:], op0=ADD, op1=ADD)
+                ph16[k], ph_push[k] = ph16_k, ph_push_k
+                if k % 2 == 1 and k + 1 < PIECES:
+                    look_up((k + 1) // 2)
 
-        def finish_drift(k, sig_blocks):
+            add_gradient(kick, q16[k][:], vw1_blocks, vb1_in, kick_v_out, True, False, nothing)
+            add_gradient(kick, p16[k][:], tw1_blocks, tb1_in, kick_t_out, False, True, finish)
+
+        def drift(k):
             speed = sums.tile([P, PIECE], F32, name="speed", tag="sum")
-            add_output(speed, drift_t_out, sig_blocks, True, True)
-            qn32 = state.tile([P, PIECE], F32, name="qn32")
-            nc.vector.tensor_tensor(qn32[:], speed[:], q16[k][:], ADD)
-            nc.sync.dma_start(out[0:P, k * PIECE : (k + 1) * PIECE], qn32[:])
-            qn16_k = state.tile([P, PIECE], BF16, name="qn16_k")
-            nc.vector.tensor_copy(qn16_k[:], qn32[:])
-            rest_k = state.tile([P, PIECE], F32, name="rest_k")
-            nc.vector.scalar_tensor_tensor(rest_k[:], speed[:], -0.5 * LAM, ph_push[k][:], op0=MULT, op1=ADD)
-            qn16[k], rest[k] = qn16_k, rest_k
 
-        def start_second_kick(k):
-            return hidden_layer(qn16[k][:], vw1_blocks, vb1_in)
+            def finish():
+                qn32 = state.tile([P, PIECE], F32, name="qn32")
+                nc.vector.tensor_tensor(qn32[:], speed[:], q16[k][:], ADD)
+                nc.sync.dma_start(out[0:P, k * PIECE : (k + 1) * PIECE], qn32[:])
+                qn16_k = state.tile([P, PIECE], BF16, name="qn16_k")
+                nc.vector.tensor_copy(qn16_k[:], qn32[:])
+                rest_k = state.tile([P, PIECE], F32, name="rest_k")
+                nc.vector.scalar_tensor_tensor(rest_k[:], speed[:], -0.5 * LAM, ph_push[k][:], op0=MULT, op1=ADD)
+                qn16[k], rest[k] = qn16_k, rest_k
 
-        def finish_second_kick(k, sig_blocks):
+            add_gradient(speed, ph16[k][:], tw1_blocks, tb1_in, drift_t_out, True, True, finish)
+
+        def second_kick(k):
             kick = sums.tile([P, PIECE], F32, name="kick", tag="sum")
-            add_output(kick, kick_v_out, sig_blocks, True, True)
-            pn32 = state.tile([P, PIECE], F32, name="pn32")
-            nc.vector.tensor_tensor(pn32[:], kick[:], rest[k][:], ADD)
-            nc.sync.dma_start(out[P : 2 * P, k * PIECE : (k + 1) * PIECE], pn32[:])
 
-        unfinished = []
+            def finish():
+                pn32 = state.tile([P, PIECE], F32, name="pn32")
+                nc.vector.tensor_tensor(pn32[:], kick[:], rest[k][:], ADD)
+                nc.sync.dma_start(out[P : 2 * P, k * PIECE : (k + 1) * PIECE], pn32[:])
 
-        def run_stage(start, finish, k):
-            sig_blocks = start(k)
-            for finish_last, k_last, sig_blocks_last in unfinished:
-                finish_last(k_last, sig_blocks_last)
-            unfinished.clear()
-            unfinished.append((finish, k, sig_blocks))
+            add_gradient(kick, qn16[k][:], vw1_blocks, vb1_in, kick_v_out, True, True, finish)
 
         look_up(0)
         for step in range(PIECES + 2):
             if step < PIECES:
-                run_stage(start_first_kick, finish_first_kick, step)
+                first_kick(step)
             if 1 <= step <= PIECES:
-                run_stage(start_drift, finish_drift, step - 1)
+                drift(step - 1)
             if step >= 2:
-                run_stage(start_second_kick, finish_second_kick, step - 2)
-        finish_second_kick(PIECES - 1, unfinished[0][2])
+                second_kick(step - 2)
+        for a in range(BLOCKS):
+            output_block(a)
+        close_unit()

@@ -16,6 +16,7 @@ TOKENS = 6144
 PIECE = 512
 PIECES = TOKENS // PIECE
 LAM = math.exp(-1.0)
+LAG = 2
 
 FLOPS = 2 * TOKENS * (P * P + 4 * 2 * P * HIDDEN)
 
@@ -30,7 +31,7 @@ def tile_latenthamiltonianpredictor_b_kernel(
         hiddens = stack.enter_context(tc.psum_pool(name="hiddens", bufs=4))
         sums = stack.enter_context(tc.psum_pool(name="sums", bufs=2))
         sigmoids = stack.enter_context(tc.tile_pool(name="sigmoids", bufs=20))
-        state = stack.enter_context(tc.tile_pool(name="state", bufs=3))
+        state = stack.enter_context(tc.tile_pool(name="state", bufs=LAG + 2))
 
         identity = held.tile([P, P], BF16, name="identity")
         make_identity(nc, identity[:])
@@ -41,29 +42,32 @@ def tile_latenthamiltonianpredictor_b_kernel(
         offsets = held.tile([P, TOKENS // 16], U16, name="offsets")
         fw_in = held.tile([P, P], BF16, name="fw_in")
         fb_in = held.tile([P, 1], F32, name="fb_in")
-        nc.sync.dma_start(q16[0][:], context[0:P, 0:PIECE])
-        nc.sync.dma_start(p16[0][:], context[P : 2 * P, 0:PIECE])
-        nc.sync.dma_start(table_rows[:], table.rearrange("(a p) e -> p a e", p=P))
-        nc.sync.dma_start(offsets[:], offs)
-        nc.sync.dma_start(fw_in[:], fw)
-        nc.sync.dma_start(fb_in[:], fb)
-        for k in range(1, PIECES):
-            cols = slice(k * PIECE, (k + 1) * PIECE)
-            nc.sync.dma_start(q16[k][:], context[0:P, cols])
-            nc.sync.dma_start(p16[k][:], context[P : 2 * P, cols])
-
         vw1_in = held.tile([P, HIDDEN], BF16, name="vw1_in")
         tw1_in = held.tile([P, HIDDEN], BF16, name="tw1_in")
         vb1_in = held.tile([P, BLOCKS], F32, name="vb1_in")
         tb1_in = held.tile([P, BLOCKS], F32, name="tb1_in")
         vw2_in = held.tile([P, BLOCKS], F32, name="vw2_in")
         tw2_in = held.tile([P, BLOCKS], F32, name="tw2_in")
+
         nc.scalar.dma_start(vw1_in[:], vw1)
         nc.scalar.dma_start(vb1_in[:], vb1.rearrange("(p a) o -> p (a o)", a=BLOCKS))
-        nc.scalar.dma_start(tw1_in[:], tw1)
-        nc.scalar.dma_start(tb1_in[:], tb1.rearrange("(p a) o -> p (a o)", a=BLOCKS))
-        nc.scalar.dma_start(vw2_in[:], vw2.rearrange("(p a) o -> p (a o)", a=BLOCKS))
-        nc.scalar.dma_start(tw2_in[:], tw2.rearrange("(p a) o -> p (a o)", a=BLOCKS))
+
+        nc.gpsimd.dma_start(fw_in[:], fw)
+        nc.gpsimd.dma_start(fb_in[:], fb)
+
+        nc.sync.dma_start(q16[0][:], context[0:P, 0:PIECE])
+        nc.sync.dma_start(vw2_in[:], vw2.rearrange("(p a) o -> p (a o)", a=BLOCKS))
+        nc.sync.dma_start(tw1_in[:], tw1)
+        nc.sync.dma_start(p16[0][:], context[P : 2 * P, 0:PIECE])
+        nc.sync.dma_start(tb1_in[:], tb1.rearrange("(p a) o -> p (a o)", a=BLOCKS))
+        nc.sync.dma_start(tw2_in[:], tw2.rearrange("(p a) o -> p (a o)", a=BLOCKS))
+        nc.sync.dma_start(table_rows[:], table.rearrange("(a p) e -> p a e", p=P))
+        nc.sync.dma_start(offsets[:], offs)
+        for k in range(1, PIECES):
+            cols = slice(k * PIECE, (k + 1) * PIECE)
+            nc.sync.dma_start(q16[k][:], context[0:P, cols])
+            nc.sync.dma_start(p16[k][:], context[P : 2 * P, cols])
+
         vw1_blocks = vw1_in[:].rearrange("d (p a) -> d a p", a=BLOCKS)
         tw1_blocks = tw1_in[:].rearrange("d (p a) -> d a p", a=BLOCKS)
 
@@ -186,13 +190,13 @@ def tile_latenthamiltonianpredictor_b_kernel(
             add_gradient(kick, qn16[k][:], vw1_blocks, vb1_in, kick_v_out, True, True, finish)
 
         look_up(0)
-        for step in range(PIECES + 2):
+        for step in range(PIECES + 2 * LAG):
             if step < PIECES:
                 first_kick(step)
-            if 1 <= step <= PIECES:
-                drift(step - 1)
-            if step >= 2:
-                second_kick(step - 2)
+            if LAG <= step < PIECES + LAG:
+                drift(step - LAG)
+            if step >= 2 * LAG:
+                second_kick(step - 2 * LAG)
         for a in range(BLOCKS):
             output_block(a)
         close_unit()

@@ -49,13 +49,12 @@ def tile_latenthamiltonianpredictor_b_kernel(
         vw2_in = held.tile([P, BLOCKS], F32, name="vw2_in")
         tw2_in = held.tile([P, BLOCKS], F32, name="tw2_in")
 
-        nc.scalar.dma_start(vw1_in[:], vw1)
-        nc.scalar.dma_start(vb1_in[:], vb1.rearrange("(p a) o -> p (a o)", a=BLOCKS))
-
         nc.gpsimd.dma_start(fw_in[:], fw)
         nc.gpsimd.dma_start(fb_in[:], fb)
 
+        nc.sync.dma_start(vw1_in[:], vw1)
         nc.sync.dma_start(q16[0][:], context[0:P, 0:PIECE])
+        nc.sync.dma_start(vb1_in[:], vb1.rearrange("(p a) o -> p (a o)", a=BLOCKS))
         nc.sync.dma_start(vw2_in[:], vw2.rearrange("(p a) o -> p (a o)", a=BLOCKS))
         nc.sync.dma_start(tw1_in[:], tw1)
         nc.sync.dma_start(p16[0][:], context[P : 2 * P, 0:PIECE])

@@ -36,6 +36,11 @@ def tile_latenthamiltonianpredictor_b_kernel(
         identity = held.tile([P, P], BF16, name="identity")
         make_identity(nc, identity[:])
 
+        zeros = held.tile([P, 1], F32, name="zeros")
+        nc.vector.memset(zeros[:], 0.0)
+        unread = held.tile([P, 1], F32, name="unread")
+        nc.scalar.activation(unread[:], zeros[:], SIGMOID)
+
         q16 = [held.tile([P, PIECE], BF16, name=f"q16_{k}") for k in range(PIECES)]
         p16 = [held.tile([P, PIECE], BF16, name=f"p16_{k}") for k in range(PIECES)]
         table_rows = held.tile([P, ACTIONS // P, P], BF16, name="table_rows")

@@ -17,6 +17,7 @@ PIECE = 512
 PIECES = TOKENS // PIECE
 LAM = math.exp(-1.0)
 LAG = 2
+LEAD = BLOCKS + 1
 
 FLOPS = 2 * TOKENS * (P * P + 4 * 2 * P * HIDDEN)
 
@@ -107,35 +108,34 @@ def tile_latenthamiltonianpredictor_b_kernel(
 
         waiting = []
 
-        def output_block(a):
-            for sig_blocks, total, w_out, first, last, after in waiting:
-                nc.tensor.matmul(
-                    total[:],
-                    w_out[:, a * P : (a + 1) * P],
-                    sig_blocks[a][:],
-                    start=first and a == 0,
-                    stop=last and a == BLOCKS - 1,
-                )
+        def output_block():
+            sig, total, w_block, start, stop, after = waiting[0]
+            waiting[:] = waiting[1:]
+            nc.tensor.matmul(total[:], w_block, sig[:], start=start, stop=stop)
+            after()
 
-        def close_unit():
-            for sig_blocks, total, w_out, first, last, after in waiting:
-                after()
-            waiting.clear()
+        def nothing():
+            return None
 
         def add_gradient(total, x16, w1_blocks, b1_in, w_out, first, last, after):
-            sig_blocks = []
             for a in range(BLOCKS):
                 hidden = hiddens.tile([P, PIECE], F32, name="hidden")
                 nc.tensor.matmul(hidden[:], w1_blocks[:, a, :], x16, start=True, stop=True)
                 sig = sigmoids.tile([P, PIECE], BF16, name="sig")
                 nc.scalar.activation(sig[:], hidden[:], SIGMOID, bias=b1_in[:, a : a + 1])
-                sig_blocks.append(sig)
-                output_block(a)
-            close_unit()
-            waiting.append((sig_blocks, total, w_out, first, last, after))
-
-        def nothing():
-            return None
+                last_block = a == BLOCKS - 1
+                waiting.append(
+                    (
+                        sig,
+                        total,
+                        w_out[:, a * P : (a + 1) * P],
+                        first and a == 0,
+                        last and last_block,
+                        after if last_block else nothing,
+                    )
+                )
+                if len(waiting) > LEAD:
+                    output_block()
 
         half_force, ph16, ph_push, qn16, rest = {}, {}, {}, {}, {}
 
@@ -153,12 +153,12 @@ def tile_latenthamiltonianpredictor_b_kernel(
             kick = sums.tile([P, PIECE], F32, name="kick", tag="sum")
 
             def finish():
-                unforced = state.tile([P, PIECE], F32, name="unforced")
-                nc.vector.tensor_tensor(unforced[:], kick[:], p16[k][:], ADD)
-                ph32 = state.tile([P, PIECE], F32, name="ph32")
-                nc.vector.scalar_tensor_tensor(ph32[:], half_force[k], fb_half[:, 0:1], unforced[:], op0=ADD, op1=ADD)
+                forced = state.tile([P, PIECE], F32, name="forced")
+                nc.vector.scalar_tensor_tensor(forced[:], half_force[k], fb_half[:, 0:1], p16[k][:], op0=ADD, op1=ADD)
                 ph16_k = state.tile([P, PIECE], BF16, name="ph16_k")
-                nc.vector.tensor_copy(ph16_k[:], ph32[:])
+                nc.vector.tensor_tensor(ph16_k[:], kick[:], forced[:], ADD)
+                ph32 = state.tile([P, PIECE], F32, name="ph32")
+                nc.vector.tensor_tensor(ph32[:], kick[:], forced[:], ADD)
                 ph_push_k = state.tile([P, PIECE], F32, name="ph_push_k")
                 nc.vector.scalar_tensor_tensor(ph_push_k[:], half_force[k], fb_half[:, 0:1], ph32[:], op0=ADD, op1=ADD)
                 ph16[k], ph_push[k] = ph16_k, ph_push_k
@@ -172,11 +172,11 @@ def tile_latenthamiltonianpredictor_b_kernel(
             speed = sums.tile([P, PIECE], F32, name="speed", tag="sum")
 
             def finish():
+                qn16_k = state.tile([P, PIECE], BF16, name="qn16_k")
+                nc.vector.tensor_tensor(qn16_k[:], speed[:], q16[k][:], ADD)
                 qn32 = state.tile([P, PIECE], F32, name="qn32")
                 nc.vector.tensor_tensor(qn32[:], speed[:], q16[k][:], ADD)
                 nc.sync.dma_start(out[0:P, k * PIECE : (k + 1) * PIECE], qn32[:])
-                qn16_k = state.tile([P, PIECE], BF16, name="qn16_k")
-                nc.vector.tensor_copy(qn16_k[:], qn32[:])
                 rest_k = state.tile([P, PIECE], F32, name="rest_k")
                 nc.vector.scalar_tensor_tensor(rest_k[:], speed[:], -0.5 * LAM, ph_push[k][:], op0=MULT, op1=ADD)
                 qn16[k], rest[k] = qn16_k, rest_k
@@ -201,6 +201,5 @@ def tile_latenthamiltonianpredictor_b_kernel(
                 drift(step - LAG)
             if step >= 2 * LAG:
                 second_kick(step - 2 * LAG)
-        for a in range(BLOCKS):
-            output_block(a)
-        close_unit()
+        for block in range(LEAD):
+            output_block()

@@ -17,7 +17,7 @@ PIECE = 512
 PIECES = TOKENS // PIECE
 LAM = math.exp(-1.0)
 LAG = 2
-LEAD = BLOCKS + 1
+LEAD = BLOCKS + 2
 
 FLOPS = 2 * TOKENS * (P * P + 4 * 2 * P * HIDDEN)
 

@@ -16,7 +16,7 @@ TOKENS = 6144
 PIECE = 512
 PIECES = TOKENS // PIECE
 LAM = math.exp(-1.0)
-LAG = 2
+FIRST_RUN = 3
 LEAD = BLOCKS + 2
 
 FLOPS = 2 * TOKENS * (P * P + 4 * 2 * P * HIDDEN)
@@ -30,9 +30,9 @@ def tile_latenthamiltonianpredictor_b_kernel(
         held = stack.enter_context(tc.tile_pool(name="held", bufs=1))
         forces = stack.enter_context(tc.psum_pool(name="forces", bufs=1))
         hiddens = stack.enter_context(tc.psum_pool(name="hiddens", bufs=4))
-        sums = stack.enter_context(tc.psum_pool(name="sums", bufs=2))
+        sums = stack.enter_context(tc.psum_pool(name="sums", bufs=3))
         sigmoids = stack.enter_context(tc.tile_pool(name="sigmoids", bufs=20))
-        state = stack.enter_context(tc.tile_pool(name="state", bufs=LAG + 2))
+        state = stack.enter_context(tc.tile_pool(name="state", bufs=4))
 
         identity = held.tile([P, P], BF16, name="identity")
         make_identity(nc, identity[:])
@@ -139,15 +139,20 @@ def tile_latenthamiltonianpredictor_b_kernel(
 
         half_force, ph16, ph_push, qn16, rest = {}, {}, {}, {}, {}
 
-        def look_up(pair):
-            force = forces.tile([P, 2, PIECE], F32, name="force")
-            for i in range(2):
-                k = 2 * pair + i
-                piece_offsets = offsets[:, k * (PIECE // 16) : (k + 1) * (PIECE // 16)]
-                nc.tensor.matmul(
-                    force[:, i, :], fw_half[:], table_cols[:].indirect(piece_offsets), start=True, stop=True
-                )
-                half_force[k] = force[:, i, :]
+        def look_up(k):
+            borrowed = k < FIRST_RUN - 1
+            if borrowed:
+                force = sums.tile([P, PIECE], F32, name="early_force", tag="sum")
+            else:
+                force = forces.tile([P, PIECE], F32, name="force")
+            piece_offsets = offsets[:, k * (PIECE // 16) : (k + 1) * (PIECE // 16)]
+            nc.tensor.matmul(force[:], fw_half[:], table_cols[:].indirect(piece_offsets), start=True, stop=True)
+            if borrowed:
+                kept = state.tile([P, PIECE], F32, name="kept")
+                nc.vector.tensor_copy(kept[:], force[:])
+                half_force[k] = kept[:]
+            else:
+                half_force[k] = force[:]
 
         def first_kick(k):
             kick = sums.tile([P, PIECE], F32, name="kick", tag="sum")
@@ -162,8 +167,8 @@ def tile_latenthamiltonianpredictor_b_kernel(
                 ph_push_k = state.tile([P, PIECE], F32, name="ph_push_k")
                 nc.vector.scalar_tensor_tensor(ph_push_k[:], half_force[k], fb_half[:, 0:1], ph32[:], op0=ADD, op1=ADD)
                 ph16[k], ph_push[k] = ph16_k, ph_push_k
-                if k % 2 == 1 and k + 1 < PIECES:
-                    look_up((k + 1) // 2)
+                if FIRST_RUN <= k + 1 < PIECES:
+                    look_up(k + 1)
 
             add_gradient(kick, q16[k][:], vw1_blocks, vb1_in, kick_v_out, True, False, nothing)
             add_gradient(kick, p16[k][:], tw1_blocks, tb1_in, kick_t_out, False, True, finish)
@@ -193,13 +198,21 @@ def tile_latenthamiltonianpredictor_b_kernel(
 
             add_gradient(kick, qn16[k][:], vw1_blocks, vb1_in, kick_v_out, True, True, finish)
 
-        look_up(0)
-        for step in range(PIECES + 2 * LAG):
-            if step < PIECES:
-                first_kick(step)
-            if LAG <= step < PIECES + LAG:
-                drift(step - LAG)
-            if step >= 2 * LAG:
-                second_kick(step - 2 * LAG)
+        for k in range(FIRST_RUN):
+            look_up(k)
+        for k in range(FIRST_RUN):
+            first_kick(k)
+        drift(0)
+        drift(1)
+        first_kick(3)
+        for step in range(4, PIECES):
+            drift(step - 2)
+            second_kick(step - 4)
+            first_kick(step)
+        drift(PIECES - 2)
+        second_kick(PIECES - 4)
+        drift(PIECES - 1)
+        for k in range(PIECES - 3, PIECES):
+            second_kick(k)
         for block in range(LEAD):
             output_block()

@@ -15,6 +15,8 @@ BLOCKS = HIDDEN // P
 TOKENS = 6144
 PIECE = 512
 PIECES = TOKENS // PIECE
+WHOLE = (slice(0, PIECE),)
+HALVES = (slice(0, PIECE // 2), slice(PIECE // 2, PIECE))
 LAM = math.exp(-1.0)
 FIRST_RUN = 3
 LEAD = BLOCKS + 2
@@ -55,19 +57,20 @@ def tile_latenthamiltonianpredictor_b_kernel(
         vw2_in = held.tile([P, BLOCKS], F32, name="vw2_in")
         tw2_in = held.tile([P, BLOCKS], F32, name="tw2_in")
 
-        nc.gpsimd.dma_start(fw_in[:], fw)
         nc.gpsimd.dma_start(fb_in[:], fb)
 
         nc.sync.dma_start(vw1_in[:], vw1)
-        nc.sync.dma_start(q16[0][:], context[0:P, 0:PIECE])
+        for cols in HALVES:
+            nc.sync.dma_start(q16[0][:, cols], context[0:P, cols])
         nc.sync.dma_start(vb1_in[:], vb1.rearrange("(p a) o -> p (a o)", a=BLOCKS))
         nc.sync.dma_start(vw2_in[:], vw2.rearrange("(p a) o -> p (a o)", a=BLOCKS))
         nc.sync.dma_start(tw1_in[:], tw1)
         nc.sync.dma_start(p16[0][:], context[P : 2 * P, 0:PIECE])
+        nc.sync.dma_start(table_rows[:], table.rearrange("(a p) e -> p a e", p=P))
+        nc.sync.dma_start(fw_in[:], fw)
+        nc.sync.dma_start(offsets[:], offs)
         nc.sync.dma_start(tb1_in[:], tb1.rearrange("(p a) o -> p (a o)", a=BLOCKS))
         nc.sync.dma_start(tw2_in[:], tw2.rearrange("(p a) o -> p (a o)", a=BLOCKS))
-        nc.sync.dma_start(table_rows[:], table.rearrange("(a p) e -> p a e", p=P))
-        nc.sync.dma_start(offsets[:], offs)
         for k in range(1, PIECES):
             cols = slice(k * PIECE, (k + 1) * PIECE)
             nc.sync.dma_start(q16[k][:], context[0:P, cols])
@@ -85,20 +88,27 @@ def tile_latenthamiltonianpredictor_b_kernel(
         gate_kick_t = held.tile([P, BLOCKS], F32, name="gate_kick_t")
         nc.vector.tensor_scalar(gate_kick_t[:], tw2_in[:], -0.5 * LAM, None, op0=MULT)
 
-        w1_flip = sums.tile([P, 2 * HIDDEN], BF16, name="w1_flip", tag="sum")
         kick_v_out = held.tile([P, HIDDEN], BF16, name="kick_v_out")
         kick_t_out = held.tile([P, HIDDEN], BF16, name="kick_t_out")
         drift_t_out = held.tile([P, HIDDEN], BF16, name="drift_t_out")
-        for a in range(BLOCKS):
-            block = slice(a * P, (a + 1) * P)
-            nc.tensor.transpose(w1_flip[:, block], vw1_blocks[:, a, :], identity[:])
-            nc.vector.tensor_scalar(kick_v_out[:, block], w1_flip[:, block], gate_kick_v[:, a : a + 1], None, op0=MULT)
-        for a in range(BLOCKS):
-            block = slice(a * P, (a + 1) * P)
-            t_block = slice(HIDDEN + a * P, HIDDEN + (a + 1) * P)
-            nc.tensor.transpose(w1_flip[:, t_block], tw1_blocks[:, a, :], identity[:])
-            nc.vector.tensor_scalar(kick_t_out[:, block], w1_flip[:, t_block], gate_kick_t[:, a : a + 1], None, op0=MULT)
-            nc.vector.tensor_scalar(drift_t_out[:, block], w1_flip[:, t_block], tw2_in[:, a : a + 1], None, op0=MULT)
+
+        def make_v_weights():
+            vw1_flip = sums.tile([P, HIDDEN], BF16, name="vw1_flip", tag="sum")
+            for a in range(BLOCKS):
+                block = slice(a * P, (a + 1) * P)
+                nc.tensor.transpose(vw1_flip[:, block], vw1_blocks[:, a, :], identity[:])
+                gate = gate_kick_v[:, a : a + 1]
+                nc.vector.tensor_scalar(kick_v_out[:, block], vw1_flip[:, block], gate, None, op0=MULT)
+
+        def make_t_weights():
+            tw1_flip = hiddens.tile([P, HIDDEN], BF16, name="tw1_flip", tag="hidden")
+            for a in range(BLOCKS):
+                block = slice(a * P, (a + 1) * P)
+                nc.tensor.transpose(tw1_flip[:, block], tw1_blocks[:, a, :], identity[:])
+                gate = gate_kick_t[:, a : a + 1]
+                nc.vector.tensor_scalar(kick_t_out[:, block], tw1_flip[:, block], gate, None, op0=MULT)
+                gate = tw2_in[:, a : a + 1]
+                nc.vector.tensor_scalar(drift_t_out[:, block], tw1_flip[:, block], gate, None, op0=MULT)
 
         table_flip = forces.tile([P, ACTIONS], BF16, name="table_flip", tag="force")
         table_cols = held.tile([P, ACTIONS], BF16, name="table_cols")
@@ -117,12 +127,14 @@ def tile_latenthamiltonianpredictor_b_kernel(
         def nothing():
             return None
 
-        def add_gradient(total, x16, w1_blocks, b1_in, w_out, first, last, after):
+        def add_gradient(total, x16, w1_blocks, b1_in, w_out, first, last, after, x_parts=WHOLE, behind=(nothing,) * BLOCKS):
             for a in range(BLOCKS):
                 hidden = hiddens.tile([P, PIECE], F32, name="hidden")
-                nc.tensor.matmul(hidden[:], w1_blocks[:, a, :], x16, start=True, stop=True)
+                for cols in x_parts:
+                    nc.tensor.matmul(hidden[:, cols], w1_blocks[:, a, :], x16[:, cols], start=True, stop=True)
                 sig = sigmoids.tile([P, PIECE], BF16, name="sig")
                 nc.scalar.activation(sig[:], hidden[:], SIGMOID, bias=b1_in[:, a : a + 1])
+                behind[a]()
                 last_block = a == BLOCKS - 1
                 waiting.append(
                     (
@@ -137,7 +149,7 @@ def tile_latenthamiltonianpredictor_b_kernel(
                 if len(waiting) > LEAD:
                     output_block()
 
-        half_force, ph16, ph_push, qn16, rest = {}, {}, {}, {}, {}
+        half_force, kick_sum, ph16, ph_push, qn16, rest = {}, {}, {}, {}, {}, {}
 
         def look_up(k):
             borrowed = k < FIRST_RUN - 1
@@ -154,8 +166,18 @@ def tile_latenthamiltonianpredictor_b_kernel(
             else:
                 half_force[k] = force[:]
 
-        def first_kick(k):
-            kick = sums.tile([P, PIECE], F32, name="kick", tag="sum")
+        def first_kick_v(k):
+            kick_sum[k] = sums.tile([P, PIECE], F32, name="kick", tag="sum")
+            if k == 0:
+                x_parts, behind = HALVES, (nothing, make_v_weights, nothing, nothing)
+            else:
+                x_parts, behind = WHOLE, (nothing,) * BLOCKS
+            add_gradient(
+                kick_sum[k], q16[k][:], vw1_blocks, vb1_in, kick_v_out, True, False, nothing, x_parts, behind
+            )
+
+        def first_kick_t(k):
+            kick = kick_sum[k]
 
             def finish():
                 forced = state.tile([P, PIECE], F32, name="forced")
@@ -170,8 +192,8 @@ def tile_latenthamiltonianpredictor_b_kernel(
                 if FIRST_RUN <= k + 1 < PIECES:
                     look_up(k + 1)
 
-            add_gradient(kick, q16[k][:], vw1_blocks, vb1_in, kick_v_out, True, False, nothing)
-            add_gradient(kick, p16[k][:], tw1_blocks, tb1_in, kick_t_out, False, True, finish)
+            behind = (make_t_weights if k == 0 else nothing, nothing, nothing, nothing)
+            add_gradient(kick, p16[k][:], tw1_blocks, tb1_in, kick_t_out, False, True, finish, WHOLE, behind)
 
         def drift(k):
             speed = sums.tile([P, PIECE], F32, name="speed", tag="sum")
@@ -201,14 +223,17 @@ def tile_latenthamiltonianpredictor_b_kernel(
         for k in range(FIRST_RUN):
             look_up(k)
         for k in range(FIRST_RUN):
-            first_kick(k)
+            first_kick_v(k)
+            first_kick_t(k)
         drift(0)
         drift(1)
-        first_kick(3)
+        first_kick_v(3)
+        first_kick_t(3)
         for step in range(4, PIECES):
             drift(step - 2)
             second_kick(step - 4)
-            first_kick(step)
+            first_kick_v(step)
+            first_kick_t(step)
         drift(PIECES - 2)
         second_kick(PIECES - 4)
         drift(PIECES - 1)

@@ -31,8 +31,8 @@ def tile_latenthamiltonianpredictor_b_kernel(
     with ExitStack() as stack:
         held = stack.enter_context(tc.tile_pool(name="held", bufs=1))
         forces = stack.enter_context(tc.psum_pool(name="forces", bufs=1))
-        hiddens = stack.enter_context(tc.psum_pool(name="hiddens", bufs=4))
-        sums = stack.enter_context(tc.psum_pool(name="sums", bufs=3))
+        hiddens = stack.enter_context(tc.psum_pool(name="hiddens", bufs=5))
+        sums = stack.enter_context(tc.psum_pool(name="sums", bufs=2))
         sigmoids = stack.enter_context(tc.tile_pool(name="sigmoids", bufs=20))
         state = stack.enter_context(tc.tile_pool(name="state", bufs=4))
 

@@ -18,7 +18,7 @@ PIECES = TOKENS // PIECE
 WHOLE = (slice(0, PIECE),)
 HALVES = (slice(0, PIECE // 2), slice(PIECE // 2, PIECE))
 LAM = math.exp(-1.0)
-FIRST_RUN = 3
+FIRST_RUN = 2
 LEAD = BLOCKS + 2
 
 FLOPS = 2 * TOKENS * (P * P + 4 * 2 * P * HIDDEN)
@@ -30,8 +30,7 @@ def tile_latenthamiltonianpredictor_b_kernel(
     nc = tc.nc
     with ExitStack() as stack:
         held = stack.enter_context(tc.tile_pool(name="held", bufs=1))
-        forces = stack.enter_context(tc.psum_pool(name="forces", bufs=1))
-        hiddens = stack.enter_context(tc.psum_pool(name="hiddens", bufs=5))
+        hiddens = stack.enter_context(tc.psum_pool(name="hiddens", bufs=6))
         sums = stack.enter_context(tc.psum_pool(name="sums", bufs=2))
         sigmoids = stack.enter_context(tc.tile_pool(name="sigmoids", bufs=20))
         state = stack.enter_context(tc.tile_pool(name="state", bufs=4))
@@ -110,7 +109,7 @@ def tile_latenthamiltonianpredictor_b_kernel(
                 gate = tw2_in[:, a : a + 1]
                 nc.vector.tensor_scalar(drift_t_out[:, block], tw1_flip[:, block], gate, None, op0=MULT)
 
-        table_flip = forces.tile([P, ACTIONS], BF16, name="table_flip", tag="force")
+        table_flip = hiddens.tile([P, ACTIONS], BF16, name="table_flip", tag="hidden")
         table_cols = held.tile([P, ACTIONS], BF16, name="table_cols")
         for a in range(ACTIONS // P):
             nc.tensor.transpose(table_flip[:, a * P : (a + 1) * P], table_rows[:, a, :], identity[:])
@@ -149,22 +148,18 @@ def tile_latenthamiltonianpredictor_b_kernel(
                 if len(waiting) > LEAD:
                     output_block()
 
-        half_force, kick_sum, ph16, ph_push, qn16, rest = {}, {}, {}, {}, {}, {}
+        push, kick_sum, ph16, ph_push, qn16, rest = {}, {}, {}, {}, {}, {}
 
         def look_up(k):
-            borrowed = k < FIRST_RUN - 1
-            if borrowed:
-                force = sums.tile([P, PIECE], F32, name="early_force", tag="sum")
+            if k < FIRST_RUN:
+                force = sums.tile([P, PIECE], F32, name="first_force", tag="sum")
             else:
-                force = forces.tile([P, PIECE], F32, name="force")
+                force = hiddens.tile([P, PIECE], F32, name="force", tag="hidden")
             piece_offsets = offsets[:, k * (PIECE // 16) : (k + 1) * (PIECE // 16)]
             nc.tensor.matmul(force[:], fw_half[:], table_cols[:].indirect(piece_offsets), start=True, stop=True)
-            if borrowed:
-                kept = state.tile([P, PIECE], F32, name="kept")
-                nc.vector.tensor_copy(kept[:], force[:])
-                half_force[k] = kept[:]
-            else:
-                half_force[k] = force[:]
+            push_k = state.tile([P, PIECE], F32, name="push_k")
+            nc.vector.tensor_scalar(push_k[:], force[:], fb_half[:, 0:1], None, op0=ADD)
+            push[k] = push_k
 
         def first_kick_v(k):
             kick_sum[k] = sums.tile([P, PIECE], F32, name="kick", tag="sum")
@@ -181,17 +176,17 @@ def tile_latenthamiltonianpredictor_b_kernel(
 
             def finish():
                 forced = state.tile([P, PIECE], F32, name="forced")
-                nc.vector.scalar_tensor_tensor(forced[:], half_force[k], fb_half[:, 0:1], p16[k][:], op0=ADD, op1=ADD)
+                nc.vector.tensor_tensor(forced[:], push[k][:], p16[k][:], ADD)
                 ph16_k = state.tile([P, PIECE], BF16, name="ph16_k")
                 nc.vector.tensor_tensor(ph16_k[:], kick[:], forced[:], ADD)
                 ph32 = state.tile([P, PIECE], F32, name="ph32")
                 nc.vector.tensor_tensor(ph32[:], kick[:], forced[:], ADD)
                 ph_push_k = state.tile([P, PIECE], F32, name="ph_push_k")
-                nc.vector.scalar_tensor_tensor(ph_push_k[:], half_force[k], fb_half[:, 0:1], ph32[:], op0=ADD, op1=ADD)
+                nc.vector.tensor_tensor(ph_push_k[:], push[k][:], ph32[:], ADD)
                 ph16[k], ph_push[k] = ph16_k, ph_push_k
-                if FIRST_RUN <= k + 1 < PIECES:
-                    look_up(k + 1)
 
+            if k >= FIRST_RUN:
+                look_up(k)
             behind = (make_t_weights if k == 0 else nothing, nothing, nothing, nothing)
             add_gradient(kick, p16[k][:], tw1_blocks, tb1_in, kick_t_out, False, True, finish, WHOLE, behind)
 
@@ -222,7 +217,7 @@ def tile_latenthamiltonianpredictor_b_kernel(
 
         for k in range(FIRST_RUN):
             look_up(k)
-        for k in range(FIRST_RUN):
+        for k in range(3):
             first_kick_v(k)
             first_kick_t(k)
         drift(0)

@@ -106,14 +106,21 @@ def tile_latenthamiltonianpredictor_b_kernel(
                 nc.tensor.transpose(tw1_flip[:, block], tw1_blocks[:, a, :], identity[:])
                 gate = gate_kick_t[:, a : a + 1]
                 nc.vector.tensor_scalar(kick_t_out[:, block], tw1_flip[:, block], gate, None, op0=MULT)
+            return tw1_flip
+
+        def make_drift_weights(tw1_flip):
+            for a in range(BLOCKS):
+                block = slice(a * P, (a + 1) * P)
                 gate = tw2_in[:, a : a + 1]
                 nc.vector.tensor_scalar(drift_t_out[:, block], tw1_flip[:, block], gate, None, op0=MULT)
 
-        table_flip = hiddens.tile([P, ACTIONS], BF16, name="table_flip", tag="hidden")
         table_cols = held.tile([P, ACTIONS], BF16, name="table_cols")
-        for a in range(ACTIONS // P):
-            nc.tensor.transpose(table_flip[:, a * P : (a + 1) * P], table_rows[:, a, :], identity[:])
-        nc.vector.tensor_copy(table_cols[:], table_flip[:])
+
+        def flip_table():
+            table_flip = hiddens.tile([P, ACTIONS], BF16, name="table_flip", tag="hidden")
+            for a in range(ACTIONS // P):
+                nc.tensor.transpose(table_flip[:, a * P : (a + 1) * P], table_rows[:, a, :], identity[:])
+            nc.vector.tensor_copy(table_cols[:], table_flip[:])
 
         waiting = []
 
@@ -149,12 +156,10 @@ def tile_latenthamiltonianpredictor_b_kernel(
                     output_block()
 
         push, kick_sum, ph16, ph_push, qn16, rest = {}, {}, {}, {}, {}, {}
+        flipped = []
 
         def look_up(k):
-            if k < FIRST_RUN:
-                force = sums.tile([P, PIECE], F32, name="first_force", tag="sum")
-            else:
-                force = hiddens.tile([P, PIECE], F32, name="force", tag="hidden")
+            force = hiddens.tile([P, PIECE], F32, name="force", tag="hidden")
             piece_offsets = offsets[:, k * (PIECE // 16) : (k + 1) * (PIECE // 16)]
             nc.tensor.matmul(force[:], fw_half[:], table_cols[:].indirect(piece_offsets), start=True, stop=True)
             push_k = state.tile([P, PIECE], F32, name="push_k")
@@ -185,9 +190,23 @@ def tile_latenthamiltonianpredictor_b_kernel(
                 nc.vector.tensor_tensor(ph_push_k[:], push[k][:], ph32[:], ADD)
                 ph16[k], ph_push[k] = ph16_k, ph_push_k
 
-            if k >= FIRST_RUN:
+            def head_t_weights():
+                flipped.append(make_t_weights())
+
+            def first_run():
+                for piece in range(FIRST_RUN):
+                    look_up(piece)
+                make_drift_weights(flipped[0])
+
+            def own_look_up():
                 look_up(k)
-            behind = (make_t_weights if k == 0 else nothing, nothing, nothing, nothing)
+
+            if k == 0:
+                behind = (flip_table, head_t_weights, first_run, nothing)
+            elif k < FIRST_RUN:
+                behind = (nothing,) * BLOCKS
+            else:
+                behind = (nothing, nothing, own_look_up, nothing)
             add_gradient(kick, p16[k][:], tw1_blocks, tb1_in, kick_t_out, False, True, finish, WHOLE, behind)
 
         def drift(k):
@@ -215,8 +234,6 @@ def tile_latenthamiltonianpredictor_b_kernel(
 
             add_gradient(kick, qn16[k][:], vw1_blocks, vb1_in, kick_v_out, True, True, finish)
 
-        for k in range(FIRST_RUN):
-            look_up(k)
         for k in range(3):
             first_kick_v(k)
             first_kick_t(k)

import math
from contextlib import ExitStack

import concourse.mybir as mybir
from concourse.masks import make_identity

BF16, F32, U16 = mybir.dt.bfloat16, mybir.dt.float32, mybir.dt.uint16
ADD, MULT = mybir.AluOpType.add, mybir.AluOpType.mult
SIGMOID = mybir.ActivationFunctionType.Sigmoid

P = 128
ACTIONS = 1024
HIDDEN = 512
BLOCKS = HIDDEN // P
TOKENS = 6144
PIECE = 512
PIECES = TOKENS // PIECE
WHOLE = (slice(0, PIECE),)
HALVES = (slice(0, PIECE // 2), slice(PIECE // 2, PIECE))
LAM = math.exp(-1.0)
FIRST_RUN = 2
LEAD = BLOCKS + 2

FLOPS = 2 * TOKENS * (P * P + 4 * 2 * P * HIDDEN)


def tile_latenthamiltonianpredictor_b_kernel(
    tc, context, table, fw, fb, tw1, tb1, tw2, vw1, vb1, vw2, offs, out
):
    nc = tc.nc
    with ExitStack() as stack:
        held = stack.enter_context(tc.tile_pool(name="held", bufs=1))
        hiddens = stack.enter_context(tc.psum_pool(name="hiddens", bufs=6))
        sums = stack.enter_context(tc.psum_pool(name="sums", bufs=2))
        sigmoids = stack.enter_context(tc.tile_pool(name="sigmoids", bufs=20))
        state = stack.enter_context(tc.tile_pool(name="state", bufs=4))

        identity = held.tile([P, P], BF16, name="identity")
        make_identity(nc, identity[:])

        zeros = held.tile([P, 1], F32, name="zeros")
        nc.vector.memset(zeros[:], 0.0)
        unread = held.tile([P, 1], F32, name="unread")
        nc.scalar.activation(unread[:], zeros[:], SIGMOID)

        q16 = [held.tile([P, PIECE], BF16, name=f"q16_{k}") for k in range(PIECES)]
        p16 = [held.tile([P, PIECE], BF16, name=f"p16_{k}") for k in range(PIECES)]
        table_rows = held.tile([P, ACTIONS // P, P], BF16, name="table_rows")
        offsets = held.tile([P, TOKENS // 16], U16, name="offsets")
        fw_in = held.tile([P, P], BF16, name="fw_in")
        fb_in = held.tile([P, 1], F32, name="fb_in")
        vw1_in = held.tile([P, HIDDEN], BF16, name="vw1_in")
        tw1_in = held.tile([P, HIDDEN], BF16, name="tw1_in")
        vb1_in = held.tile([P, BLOCKS], F32, name="vb1_in")
        tb1_in = held.tile([P, BLOCKS], F32, name="tb1_in")
        vw2_in = held.tile([P, BLOCKS], F32, name="vw2_in")
        tw2_in = held.tile([P, BLOCKS], F32, name="tw2_in")

        nc.gpsimd.dma_start(fb_in[:], fb)

        nc.sync.dma_start(vw1_in[:], vw1)
        for cols in HALVES:
            nc.sync.dma_start(q16[0][:, cols], context[0:P, cols])
        nc.sync.dma_start(vb1_in[:], vb1.rearrange("(p a) o -> p (a o)", a=BLOCKS))
        nc.sync.dma_start(vw2_in[:], vw2.rearrange("(p a) o -> p (a o)", a=BLOCKS))
        nc.sync.dma_start(tw1_in[:], tw1)
        nc.sync.dma_start(p16[0][:], context[P : 2 * P, 0:PIECE])
        nc.sync.dma_start(table_rows[:], table.rearrange("(a p) e -> p a e", p=P))
        nc.sync.dma_start(fw_in[:], fw)
        nc.sync.dma_start(offsets[:], offs)
        nc.sync.dma_start(tb1_in[:], tb1.rearrange("(p a) o -> p (a o)", a=BLOCKS))
        nc.sync.dma_start(tw2_in[:], tw2.rearrange("(p a) o -> p (a o)", a=BLOCKS))
        for k in range(1, PIECES):
            cols = slice(k * PIECE, (k + 1) * PIECE)
            nc.sync.dma_start(q16[k][:], context[0:P, cols])
            nc.sync.dma_start(p16[k][:], context[P : 2 * P, cols])

        vw1_blocks = vw1_in[:].rearrange("d (p a) -> d a p", a=BLOCKS)
        tw1_blocks = tw1_in[:].rearrange("d (p a) -> d a p", a=BLOCKS)

        fw_half = held.tile([P, P], BF16, name="fw_half")
        nc.vector.tensor_scalar(fw_half[:], fw_in[:], 0.5, None, op0=MULT)
        fb_half = held.tile([P, 1], F32, name="fb_half")
        nc.vector.tensor_scalar(fb_half[:], fb_in[:], 0.5, None, op0=MULT)
        gate_kick_v = held.tile([P, BLOCKS], F32, name="gate_kick_v")
        nc.vector.tensor_scalar(gate_kick_v[:], vw2_in[:], -0.5, None, op0=MULT)
        gate_kick_t = held.tile([P, BLOCKS], F32, name="gate_kick_t")
        nc.vector.tensor_scalar(gate_kick_t[:], tw2_in[:], -0.5 * LAM, None, op0=MULT)

        kick_v_out = held.tile([P, HIDDEN], BF16, name="kick_v_out")
        kick_t_out = held.tile([P, HIDDEN], BF16, name="kick_t_out")
        drift_t_out = held.tile([P, HIDDEN], BF16, name="drift_t_out")

        def make_v_weights():
            vw1_flip = sums.tile([P, HIDDEN], BF16, name="vw1_flip", tag="sum")
            for a in range(BLOCKS):
                block = slice(a * P, (a + 1) * P)
                nc.tensor.transpose(vw1_flip[:, block], vw1_blocks[:, a, :], identity[:])
                gate = gate_kick_v[:, a : a + 1]
                nc.vector.tensor_scalar(kick_v_out[:, block], vw1_flip[:, block], gate, None, op0=MULT)

        def make_t_weights():
            tw1_flip = hiddens.tile([P, HIDDEN], BF16, name="tw1_flip", tag="hidden")
            for a in range(BLOCKS):
                block = slice(a * P, (a + 1) * P)
                nc.tensor.transpose(tw1_flip[:, block], tw1_blocks[:, a, :], identity[:])
                gate = gate_kick_t[:, a : a + 1]
                nc.vector.tensor_scalar(kick_t_out[:, block], tw1_flip[:, block], gate, None, op0=MULT)
            return tw1_flip

        def make_drift_weights(tw1_flip):
            for a in range(BLOCKS):
                block = slice(a * P, (a + 1) * P)
                gate = tw2_in[:, a : a + 1]
                nc.vector.tensor_scalar(drift_t_out[:, block], tw1_flip[:, block], gate, None, op0=MULT)

        table_cols = held.tile([P, ACTIONS], BF16, name="table_cols")

        def flip_table():
            table_flip = hiddens.tile([P, ACTIONS], BF16, name="table_flip", tag="hidden")
            for a in range(ACTIONS // P):
                nc.tensor.transpose(table_flip[:, a * P : (a + 1) * P], table_rows[:, a, :], identity[:])
            nc.vector.tensor_copy(table_cols[:], table_flip[:])

        waiting = []

        def output_block():
            sig, total, w_block, start, stop, after = waiting[0]
            waiting[:] = waiting[1:]
            nc.tensor.matmul(total[:], w_block, sig[:], start=start, stop=stop)
            after()

        def nothing():
            return None

        def add_gradient(total, x16, w1_blocks, b1_in, w_out, first, last, after, x_parts=WHOLE, behind=(nothing,) * BLOCKS):
            for a in range(BLOCKS):
                hidden = hiddens.tile([P, PIECE], F32, name="hidden")
                for cols in x_parts:
                    nc.tensor.matmul(hidden[:, cols], w1_blocks[:, a, :], x16[:, cols], start=True, stop=True)
                sig = sigmoids.tile([P, PIECE], BF16, name="sig")
                nc.scalar.activation(sig[:], hidden[:], SIGMOID, bias=b1_in[:, a : a + 1])
                behind[a]()
                last_block = a == BLOCKS - 1
                waiting.append(
                    (
                        sig,
                        total,
                        w_out[:, a * P : (a + 1) * P],
                        first and a == 0,
                        last and last_block,
                        after if last_block else nothing,
                    )
                )
                if len(waiting) > LEAD:
                    output_block()

        push, kick_sum, ph16, ph_push, qn16, rest = {}, {}, {}, {}, {}, {}
        flipped = []

        def look_up(k):
            force = hiddens.tile([P, PIECE], F32, name="force", tag="hidden")
            piece_offsets = offsets[:, k * (PIECE // 16) : (k + 1) * (PIECE // 16)]
            nc.tensor.matmul(force[:], fw_half[:], table_cols[:].indirect(piece_offsets), start=True, stop=True)
            push_k = state.tile([P, PIECE], F32, name="push_k")
            nc.vector.tensor_scalar(push_k[:], force[:], fb_half[:, 0:1], None, op0=ADD)
            push[k] = push_k

        def first_kick_v(k):
            kick_sum[k] = sums.tile([P, PIECE], F32, name="kick", tag="sum")
            if k == 0:
                x_parts, behind = HALVES, (nothing, make_v_weights, nothing, nothing)
            else:
                x_parts, behind = WHOLE, (nothing,) * BLOCKS
            add_gradient(
                kick_sum[k], q16[k][:], vw1_blocks, vb1_in, kick_v_out, True, False, nothing, x_parts, behind
            )

        def first_kick_t(k):
            kick = kick_sum[k]

            def finish():
                forced = state.tile([P, PIECE], F32, name="forced")
                nc.vector.tensor_tensor(forced[:], push[k][:], p16[k][:], ADD)
                ph16_k = state.tile([P, PIECE], BF16, name="ph16_k")
                nc.vector.tensor_tensor(ph16_k[:], kick[:], forced[:], ADD)
                ph32 = state.tile([P, PIECE], F32, name="ph32")
                nc.vector.tensor_tensor(ph32[:], kick[:], forced[:], ADD)
                ph_push_k = state.tile([P, PIECE], F32, name="ph_push_k")
                nc.vector.tensor_tensor(ph_push_k[:], push[k][:], ph32[:], ADD)
                ph16[k], ph_push[k] = ph16_k, ph_push_k

            def head_t_weights():
                flipped.append(make_t_weights())

            def first_run():
                for piece in range(FIRST_RUN):
                    look_up(piece)
                make_drift_weights(flipped[0])

            def own_look_up():
                look_up(k)

            if k == 0:
                behind = (flip_table, head_t_weights, first_run, nothing)
            elif k < FIRST_RUN:
                behind = (nothing,) * BLOCKS
            else:
                behind = (nothing, nothing, own_look_up, nothing)
            add_gradient(kick, p16[k][:], tw1_blocks, tb1_in, kick_t_out, False, True, finish, WHOLE, behind)

        def drift(k):
            speed = sums.tile([P, PIECE], F32, name="speed", tag="sum")

            def finish():
                qn16_k = state.tile([P, PIECE], BF16, name="qn16_k")
                nc.vector.tensor_tensor(qn16_k[:], speed[:], q16[k][:], ADD)
                qn32 = state.tile([P, PIECE], F32, name="qn32")
                nc.vector.tensor_tensor(qn32[:], speed[:], q16[k][:], ADD)
                nc.sync.dma_start(out[0:P, k * PIECE : (k + 1) * PIECE], qn32[:])
                rest_k = state.tile([P, PIECE], F32, name="rest_k")
                nc.vector.scalar_tensor_tensor(rest_k[:], speed[:], -0.5 * LAM, ph_push[k][:], op0=MULT, op1=ADD)
                qn16[k], rest[k] = qn16_k, rest_k

            add_gradient(speed, ph16[k][:], tw1_blocks, tb1_in, drift_t_out, True, True, finish)

        def second_kick(k):
            kick = sums.tile([P, PIECE], F32, name="kick", tag="sum")

            def finish():
                pn32 = state.tile([P, PIECE], F32, name="pn32")
                nc.vector.tensor_tensor(pn32[:], kick[:], rest[k][:], ADD)
                nc.sync.dma_start(out[P : 2 * P, k * PIECE : (k + 1) * PIECE], pn32[:])

            add_gradient(kick, qn16[k][:], vw1_blocks, vb1_in, kick_v_out, True, True, finish)

        for k in range(3):
            first_kick_v(k)
            first_kick_t(k)
        drift(0)
        drift(1)
        first_kick_v(3)
        first_kick_t(3)
        for step in range(4, PIECES):
            drift(step - 2)
            second_kick(step - 4)
            first_kick_v(step)
            first_kick_t(step)
        drift(PIECES - 2)
        second_kick(PIECES - 4)
        drift(PIECES - 1)
        for k in range(PIECES - 3, PIECES):
            second_kick(k)
        for block in range(LEAD):
            output_block()
